import numpy as np
import ml_dtypes

BF16 = ml_dtypes.bfloat16


def bf(x):
    return np.asarray(x, np.float32).astype(BF16)


def f32(x):
    return np.asarray(x, np.float32)


def f64(x):
    return np.asarray(x).astype(np.float64)


def striped(idx):
    return np.tile(idx.reshape(-1, 16).T, (8, 1))


C, S, M, K, N = 512, 4096, 512, 16, 8192
SCALE = 4.9
WSTD = 0.1


def sigmoid(v):
    return 1.0 / (1.0 + np.exp(-v))


def setup_inputs():
    return {"x": f32(np.random.standard_normal((C, S))), "w": f32(WSTD * np.random.standard_normal((1, N))), "offs": striped(np.random.permutation(np.tile(np.arange(S), 2))[:N])}


def reference(x, w, offs):
    idx = offs[:16].T.reshape(-1)
    prod = f64(x)[:, idx] * f64(w)
    pre = SCALE * prod.reshape(C, M, K).sum(axis=2)
    return sigmoid(pre)

@@ -1,0 +1,52 @@
+import concourse.mybir as mybir
+
+F32 = mybir.dt.float32
+U16 = mybir.dt.uint16
+
+P = 128
+C, S, M, K = 512, 4096, 512, 16
+N = M * K
+SCALE = 4.9
+PIECE = 4096
+NODES = PIECE // K
+FLOPS = 2 * C * N
+
+
+def tile_feedforwardnetwork_kernel(tc, x, w, offs, out):
+    nc = tc.nc
+    with (
+        tc.tile_pool(name="held", bufs=1) as held,
+        tc.tile_pool(name="work", bufs=2) as work,
+    ):
+        offsets = held.tile([P, N // 16], U16, name="offsets")
+        nc.sync.dma_start(offsets[:], offs)
+        weights = held.tile([P, N], F32, name="weights")
+        nc.sync.dma_start(weights[:], w.broadcast_to([P, N]))
+
+        for b in range(C // P):
+            table = held.tile([P, S], F32, name=f"table{b}")
+            nc.sync.dma_start(table[:], x[b * P : (b + 1) * P, :])
+            result = work.tile([P, M], F32, name="result")
+            for piece in range(N // PIECE):
+                first = piece * PIECE
+                products = work.tile([P, PIECE], F32, name="products")
+                nc.vector.tensor_tensor(
+                    products[:],
+                    table[:].indirect(offsets[:, first // 16 : (first + PIECE) // 16]),
+                    weights[:, first : first + PIECE],
+                    mybir.AluOpType.mult,
+                )
+                sums = work.tile([P, NODES], F32, name="sums")
+                nc.vector.tensor_reduce(
+                    out=sums[:],
+                    in_=products[:].rearrange("p (m k) -> p m k", k=K),
+                    axis=mybir.AxisListType.X,
+                    op=mybir.AluOpType.add,
+                )
+                nc.scalar.activation(
+                    result[:, piece * NODES : (piece + 1) * NODES],
+                    sums[:],
+                    mybir.ActivationFunctionType.Sigmoid,
+                    scale=SCALE,
+                )
+            nc.sync.dma_start(out[b * P : (b + 1) * P, :], result[:])

@@ -1,4 +1,5 @@
 import concourse.mybir as mybir
+from concourse.masks import make_identity
 
 F32 = mybir.dt.float32
 U16 = mybir.dt.uint16
@@ -7,8 +8,8 @@ P = 128
 C, S, M, K = 512, 4096, 512, 16
 N = M * K
 SCALE = 4.9
-PIECE = 4096
-NODES = PIECE // K
+NODES = P
+PIECE = NODES * K
 FLOPS = 2 * C * N
 
 
@@ -16,37 +17,54 @@ def tile_feedforwardnetwork_kernel(tc, x, w, offs, out):
     nc = tc.nc
     with (
         tc.tile_pool(name="held", bufs=1) as held,
-        tc.tile_pool(name="work", bufs=2) as work,
+        tc.tile_pool(name="work", bufs=3) as work,
+        tc.psum_pool(name="psum", bufs=2) as psum,
     ):
         offsets = held.tile([P, N // 16], U16, name="offsets")
         nc.sync.dma_start(offsets[:], offs)
-        weights = held.tile([P, N], F32, name="weights")
-        nc.sync.dma_start(weights[:], w.broadcast_to([P, N]))
+        weights = [held.tile([P, PIECE], F32, name=f"weights{piece}") for piece in range(N // PIECE)]
+        tables = [held.tile([P, S], F32, name=f"table{b}") for b in range(C // P)]
+        nc.sync.dma_start(weights[0][:], w[:, 0:PIECE].broadcast_to([P, PIECE]))
+        nc.sync.dma_start(tables[0][:], x[0:P, :])
+        for piece in range(1, N // PIECE):
+            nc.sync.dma_start(
+                weights[piece][:], w[:, piece * PIECE : (piece + 1) * PIECE].broadcast_to([P, PIECE])
+            )
+        for b in range(1, C // P):
+            nc.sync.dma_start(tables[b][:], x[b * P : (b + 1) * P, :])
+
+        identity = held.tile([P, P], F32, name="identity")
+        make_identity(nc, identity[:])
 
         for b in range(C // P):
-            table = held.tile([P, S], F32, name=f"table{b}")
-            nc.sync.dma_start(table[:], x[b * P : (b + 1) * P, :])
-            result = work.tile([P, M], F32, name="result")
             for piece in range(N // PIECE):
                 first = piece * PIECE
                 products = work.tile([P, PIECE], F32, name="products")
                 nc.vector.tensor_tensor(
                     products[:],
-                    table[:].indirect(offsets[:, first // 16 : (first + PIECE) // 16]),
-                    weights[:, first : first + PIECE],
+                    tables[b][:].indirect(offsets[:, first // 16 : (first + PIECE) // 16]),
+                    weights[piece][:],
                     mybir.AluOpType.mult,
                 )
-                sums = work.tile([P, NODES], F32, name="sums")
-                nc.vector.tensor_reduce(
-                    out=sums[:],
-                    in_=products[:].rearrange("p (m k) -> p m k", k=K),
-                    axis=mybir.AxisListType.X,
-                    op=mybir.AluOpType.add,
-                )
+                by_edge = products[:].rearrange("p (m k) -> p k m", k=K)
+                sums_by_node = psum.tile([NODES, P], F32, name="sums_by_node")
+                for k in range(K):
+                    nc.tensor.matmul(
+                        sums_by_node[:],
+                        lhsT=by_edge[:, k, :],
+                        rhs=identity[:],
+                        is_transpose=True,
+                        start=(k == 0),
+                        stop=(k == K - 1),
+                    )
+                sums_copy = work.tile([NODES, P], F32, name="sums_copy")
+                nc.scalar.copy(sums_copy[:], sums_by_node[:])
+                sums = psum.tile([P, NODES], F32, name="sums")
+                nc.tensor.transpose(sums[:], sums_copy[:], identity[:])
+                result = work.tile([P, NODES], F32, name="result")
                 nc.scalar.activation(
-                    result[:, piece * NODES : (piece + 1) * NODES],
-                    sums[:],
-                    mybir.ActivationFunctionType.Sigmoid,
-                    scale=SCALE,
+                    result[:], sums[:], mybir.ActivationFunctionType.Sigmoid, scale=SCALE
                 )
-            nc.sync.dma_start(out[b * P : (b + 1) * P, :], result[:])
+                nc.sync.dma_start(
+                    out[b * P : (b + 1) * P, piece * NODES : (piece + 1) * NODES], result[:]
+                )

@@ -46,21 +46,30 @@ def tile_feedforwardnetwork_kernel(tc, x, w, offs, out):
                     weights[piece][:],
                     mybir.AluOpType.mult,
                 )
-                by_edge = products[:].rearrange("p (m k) -> p k m", k=K)
-                sums_by_node = psum.tile([NODES, P], F32, name="sums_by_node")
-                for k in range(K):
-                    nc.tensor.matmul(
-                        sums_by_node[:],
-                        lhsT=by_edge[:, k, :],
-                        rhs=identity[:],
-                        is_transpose=True,
-                        start=(k == 0),
-                        stop=(k == K - 1),
+                if b == C // P - 1 and piece == N // PIECE - 1:
+                    sums = work.tile([P, NODES], F32, name="last_sums")
+                    nc.vector.tensor_reduce(
+                        out=sums[:],
+                        in_=products[:].rearrange("p (m k) -> p m k", k=K),
+                        axis=mybir.AxisListType.X,
+                        op=mybir.AluOpType.add,
                     )
-                sums_copy = work.tile([NODES, P], F32, name="sums_copy")
-                nc.scalar.copy(sums_copy[:], sums_by_node[:])
-                sums = psum.tile([P, NODES], F32, name="sums")
-                nc.tensor.transpose(sums[:], sums_copy[:], identity[:])
+                else:
+                    by_edge = products[:].rearrange("p (m k) -> p k m", k=K)
+                    sums_by_node = psum.tile([NODES, P], F32, name="sums_by_node")
+                    for k in range(K):
+                        nc.tensor.matmul(
+                            sums_by_node[:],
+                            lhsT=by_edge[:, k, :],
+                            rhs=identity[:],
+                            is_transpose=True,
+                            start=(k == 0),
+                            stop=(k == K - 1),
+                        )
+                    sums_copy = work.tile([NODES, P], F32, name="sums_copy")
+                    nc.scalar.copy(sums_copy[:], sums_by_node[:])
+                    sums = psum.tile([P, NODES], F32, name="sums")
+                    nc.tensor.transpose(sums[:], sums_copy[:], identity[:])
                 result = work.tile([P, NODES], F32, name="result")
                 nc.scalar.activation(
                     result[:], sums[:], mybir.ActivationFunctionType.Sigmoid, scale=SCALE

@@ -10,6 +10,7 @@ N = M * K
 SCALE = 4.9
 NODES = P
 PIECE = NODES * K
+HEAD = PIECE // 4
 FLOPS = 2 * C * N
 
 
@@ -24,8 +25,9 @@ def tile_feedforwardnetwork_kernel(tc, x, w, offs, out):
         nc.sync.dma_start(offsets[:], offs)
         weights = [held.tile([P, PIECE], F32, name=f"weights{piece}") for piece in range(N // PIECE)]
         tables = [held.tile([P, S], F32, name=f"table{b}") for b in range(C // P)]
-        nc.sync.dma_start(weights[0][:], w[:, 0:PIECE].broadcast_to([P, PIECE]))
+        nc.sync.dma_start(weights[0][:, 0:HEAD], w[:, 0:HEAD].broadcast_to([P, HEAD]))
         nc.sync.dma_start(tables[0][:], x[0:P, :])
+        nc.sync.dma_start(weights[0][:, HEAD:PIECE], w[:, HEAD:PIECE].broadcast_to([P, PIECE - HEAD]))
         for piece in range(1, N // PIECE):
             nc.sync.dma_start(
                 weights[piece][:], w[:, piece * PIECE : (piece + 1) * PIECE].broadcast_to([P, PIECE])
@@ -40,12 +42,14 @@ def tile_feedforwardnetwork_kernel(tc, x, w, offs, out):
             for piece in range(N // PIECE):
                 first = piece * PIECE
                 products = work.tile([P, PIECE], F32, name="products")
-                nc.vector.tensor_tensor(
-                    products[:],
-                    tables[b][:].indirect(offsets[:, first // 16 : (first + PIECE) // 16]),
-                    weights[piece][:],
-                    mybir.AluOpType.mult,
-                )
+                cuts = [0, HEAD, PIECE] if b == 0 and piece == 0 else [0, PIECE]
+                for lo, hi in zip(cuts[:-1], cuts[1:]):
+                    nc.vector.tensor_tensor(
+                        products[:, lo:hi],
+                        tables[b][:].indirect(offsets[:, (first + lo) // 16 : (first + hi) // 16]),
+                        weights[piece][:, lo:hi],
+                        mybir.AluOpType.mult,
+                    )
                 if b == C // P - 1 and piece == N // PIECE - 1:
                     sums = work.tile([P, NODES], F32, name="last_sums")
                     nc.vector.tensor_reduce(

@@ -10,7 +10,8 @@ N = M * K
 SCALE = 4.9
 NODES = P
 PIECE = NODES * K
-HEAD = PIECE // 4
+BANK = 512
+HEAD = BANK
 FLOPS = 2 * C * N
 
 
@@ -20,23 +21,39 @@ def tile_feedforwardnetwork_kernel(tc, x, w, offs, out):
         tc.tile_pool(name="held", bufs=1) as held,
         tc.tile_pool(name="work", bufs=3) as work,
         tc.psum_pool(name="psum", bufs=2) as psum,
+        tc.psum_pool(name="psum_once", bufs=1) as psum_once,
     ):
         offsets = held.tile([P, N // 16], U16, name="offsets")
         nc.sync.dma_start(offsets[:], offs)
-        weights = [held.tile([P, PIECE], F32, name=f"weights{piece}") for piece in range(N // PIECE)]
+        weight_rows = held.tile([N // P, P], F32, name="weight_rows")
+        nc.sync.dma_start(weight_rows[:], w.rearrange("o (q f) -> (o q) f", f=P))
         tables = [held.tile([P, S], F32, name=f"table{b}") for b in range(C // P)]
-        nc.sync.dma_start(weights[0][:, 0:HEAD], w[:, 0:HEAD].broadcast_to([P, HEAD]))
-        nc.sync.dma_start(tables[0][:], x[0:P, :])
-        nc.sync.dma_start(weights[0][:, HEAD:PIECE], w[:, HEAD:PIECE].broadcast_to([P, PIECE - HEAD]))
-        for piece in range(1, N // PIECE):
-            nc.sync.dma_start(
-                weights[piece][:], w[:, piece * PIECE : (piece + 1) * PIECE].broadcast_to([P, PIECE])
-            )
-        for b in range(1, C // P):
+        for b in range(C // P):
             nc.sync.dma_start(tables[b][:], x[b * P : (b + 1) * P, :])
 
         identity = held.tile([P, P], F32, name="identity")
         make_identity(nc, identity[:])
+
+        turned = psum_once.tile([P, N // P], F32, name="turned")
+        nc.tensor.transpose(turned[:], weight_rows[:], identity[0 : N // P, 0 : N // P])
+        weight_columns = held.tile([P, N // P], F32, name="weight_columns")
+        nc.scalar.copy(weight_columns[:], turned[:])
+
+        weights = [held.tile([P, PIECE], F32, name=f"weights{piece}") for piece in range(N // PIECE)]
+        for piece in range(N // PIECE):
+            for bank in range(PIECE // BANK):
+                spread = psum.tile([P, BANK], F32, name="spread")
+                for part in range(BANK // P):
+                    q = (piece * PIECE + bank * BANK) // P + part
+                    nc.tensor.matmul(
+                        spread[:, part * P : (part + 1) * P],
+                        lhsT=weight_columns[:, q : q + 1].to_broadcast([P, P]),
+                        rhs=identity[:],
+                        is_transpose=True,
+                        start=True,
+                        stop=True,
+                    )
+                nc.scalar.copy(weights[piece][:, bank * BANK : (bank + 1) * BANK], spread[:])
 
         for b in range(C // P):
             for piece in range(N // PIECE):

@@ -9,10 +9,18 @@ C, S, M, K = 512, 4096, 512, 16
 N = M * K
 SCALE = 4.9
 NODES = P
-PIECE = NODES * K
+UNIT = NODES * K
+SPAN = 2 * UNIT
 BANK = 512
-HEAD = BANK
 FLOPS = 2 * C * N
+
+
+def steps_of(b, span):
+    if b == 0 and span == 0:
+        return [0, BANK, UNIT, SPAN]
+    if b == 0 or (b == C // P - 1 and span == N // SPAN - 1):
+        return [0, UNIT, SPAN]
+    return [0, SPAN]
 
 
 def tile_feedforwardnetwork_kernel(tc, x, w, offs, out):
@@ -39,12 +47,12 @@ def tile_feedforwardnetwork_kernel(tc, x, w, offs, out):
         weight_columns = held.tile([P, N // P], F32, name="weight_columns")
         nc.scalar.copy(weight_columns[:], turned[:])
 
-        weights = [held.tile([P, PIECE], F32, name=f"weights{piece}") for piece in range(N // PIECE)]
-        for piece in range(N // PIECE):
-            for bank in range(PIECE // BANK):
+        weights = [held.tile([P, SPAN], F32, name=f"weights{span}") for span in range(N // SPAN)]
+        for span in range(N // SPAN):
+            for bank in range(SPAN // BANK):
                 spread = psum.tile([P, BANK], F32, name="spread")
                 for part in range(BANK // P):
-                    q = (piece * PIECE + bank * BANK) // P + part
+                    q = (span * SPAN + bank * BANK) // P + part
                     nc.tensor.matmul(
                         spread[:, part * P : (part + 1) * P],
                         lhsT=weight_columns[:, q : q + 1].to_broadcast([P, P]),
@@ -53,48 +61,50 @@ def tile_feedforwardnetwork_kernel(tc, x, w, offs, out):
                         start=True,
                         stop=True,
                     )
-                nc.scalar.copy(weights[piece][:, bank * BANK : (bank + 1) * BANK], spread[:])
+                nc.scalar.copy(weights[span][:, bank * BANK : (bank + 1) * BANK], spread[:])
 
         for b in range(C // P):
-            for piece in range(N // PIECE):
-                first = piece * PIECE
-                products = work.tile([P, PIECE], F32, name="products")
-                cuts = [0, HEAD, PIECE] if b == 0 and piece == 0 else [0, PIECE]
-                for lo, hi in zip(cuts[:-1], cuts[1:]):
+            for span in range(N // SPAN):
+                products = work.tile([P, SPAN], F32, name="products")
+                steps = steps_of(b, span)
+                for lo, hi in zip(steps[:-1], steps[1:]):
                     nc.vector.tensor_tensor(
                         products[:, lo:hi],
-                        tables[b][:].indirect(offsets[:, (first + lo) // 16 : (first + hi) // 16]),
-                        weights[piece][:, lo:hi],
+                        tables[b][:].indirect(offsets[:, (span * SPAN + lo) // 16 : (span * SPAN + hi) // 16]),
+                        weights[span][:, lo:hi],
                         mybir.AluOpType.mult,
                     )
-                if b == C // P - 1 and piece == N // PIECE - 1:
-                    sums = work.tile([P, NODES], F32, name="last_sums")
-                    nc.vector.tensor_reduce(
-                        out=sums[:],
-                        in_=products[:].rearrange("p (m k) -> p m k", k=K),
-                        axis=mybir.AxisListType.X,
-                        op=mybir.AluOpType.add,
-                    )
-                else:
-                    by_edge = products[:].rearrange("p (m k) -> p k m", k=K)
-                    sums_by_node = psum.tile([NODES, P], F32, name="sums_by_node")
-                    for k in range(K):
-                        nc.tensor.matmul(
-                            sums_by_node[:],
-                            lhsT=by_edge[:, k, :],
-                            rhs=identity[:],
-                            is_transpose=True,
-                            start=(k == 0),
-                            stop=(k == K - 1),
+                for unit in range(SPAN // UNIT):
+                    of_unit = products[:, unit * UNIT : (unit + 1) * UNIT]
+                    first_node = (span * SPAN + unit * UNIT) // K
+                    if b == C // P - 1 and first_node == M - NODES:
+                        sums = work.tile([P, NODES], F32, name="last_sums")
+                        nc.vector.tensor_reduce(
+                            out=sums[:],
+                            in_=of_unit.rearrange("p (m k) -> p m k", k=K),
+                            axis=mybir.AxisListType.X,
+                            op=mybir.AluOpType.add,
                         )
-                    sums_copy = work.tile([NODES, P], F32, name="sums_copy")
-                    nc.scalar.copy(sums_copy[:], sums_by_node[:])
-                    sums = psum.tile([P, NODES], F32, name="sums")
-                    nc.tensor.transpose(sums[:], sums_copy[:], identity[:])
-                result = work.tile([P, NODES], F32, name="result")
-                nc.scalar.activation(
-                    result[:], sums[:], mybir.ActivationFunctionType.Sigmoid, scale=SCALE
-                )
-                nc.sync.dma_start(
-                    out[b * P : (b + 1) * P, piece * NODES : (piece + 1) * NODES], result[:]
-                )
+                    else:
+                        by_edge = of_unit.rearrange("p (m k) -> p k m", k=K)
+                        sums_by_node = psum.tile([NODES, P], F32, name="sums_by_node")
+                        for k in range(K):
+                            nc.tensor.matmul(
+                                sums_by_node[:],
+                                lhsT=by_edge[:, k, :],
+                                rhs=identity[:],
+                                is_transpose=True,
+                                start=(k == 0),
+                                stop=(k == K - 1),
+                            )
+                        sums_copy = work.tile([NODES, P], F32, name="sums_copy")
+                        nc.scalar.copy(sums_copy[:], sums_by_node[:])
+                        sums = psum.tile([P, NODES], F32, name="sums")
+                        nc.tensor.transpose(sums[:], sums_copy[:], identity[:])
+                    result = work.tile([P, NODES], F32, name="result")
+                    nc.scalar.activation(
+                        result[:], sums[:], mybir.ActivationFunctionType.Sigmoid, scale=SCALE
+                    )
+                    nc.sync.dma_start(
+                        out[b * P : (b + 1) * P, first_node : first_node + NODES], result[:]
+                    )

@@ -105,6 +105,6 @@ def tile_feedforwardnetwork_kernel(tc, x, w, offs, out):
                     nc.scalar.activation(
                         result[:], sums[:], mybir.ActivationFunctionType.Sigmoid, scale=SCALE
                     )
-                    nc.sync.dma_start(
+                    nc.scalar.dma_start(
                         out[b * P : (b + 1) * P, first_node : first_node + NODES], result[:]
                     )

@@ -18,7 +18,7 @@ FLOPS = 2 * C * N
 def steps_of(b, span):
     if b == 0 and span == 0:
         return [0, BANK, UNIT, SPAN]
-    if b == 0 or (b == C // P - 1 and span == N // SPAN - 1):
+    if b == C // P - 1 and span == N // SPAN - 1:
         return [0, UNIT, SPAN]
     return [0, SPAN]
 
@@ -63,8 +63,8 @@ def tile_feedforwardnetwork_kernel(tc, x, w, offs, out):
                     )
                 nc.scalar.copy(weights[span][:, bank * BANK : (bank + 1) * BANK], spread[:])
 
-        for b in range(C // P):
-            for span in range(N // SPAN):
+        for span in range(N // SPAN):
+            for b in range(C // P):
                 products = work.tile([P, SPAN], F32, name="products")
                 steps = steps_of(b, span)
                 for lo, hi in zip(steps[:-1], steps[1:]):

@@ -12,6 +12,7 @@ NODES = P
 UNIT = NODES * K
 SPAN = 2 * UNIT
 BANK = 512
+HELPED = 24
 FLOPS = 2 * C * N
 
 
@@ -78,12 +79,29 @@ def tile_feedforwardnetwork_kernel(tc, x, w, offs, out):
                     of_unit = products[:, unit * UNIT : (unit + 1) * UNIT]
                     first_node = (span * SPAN + unit * UNIT) // K
                     if b == C // P - 1 and first_node == M - NODES:
+                        by_node = of_unit.rearrange("p (m k) -> p m k", k=K)
                         sums = work.tile([P, NODES], F32, name="last_sums")
                         nc.vector.tensor_reduce(
-                            out=sums[:],
-                            in_=of_unit.rearrange("p (m k) -> p m k", k=K),
+                            out=sums[:, 0 : NODES - HELPED],
+                            in_=by_node[:, 0 : NODES - HELPED, :],
                             axis=mybir.AxisListType.X,
                             op=mybir.AluOpType.add,
+                        )
+                        halved = by_node[:, NODES - HELPED : NODES, :]
+                        for width in (8, 4, 2):
+                            folded = work.tile([P, HELPED, width], F32, name=f"folded{width}")
+                            nc.gpsimd.tensor_tensor(
+                                folded[:],
+                                halved[:, :, 0:width],
+                                halved[:, :, width : 2 * width],
+                                mybir.AluOpType.add,
+                            )
+                            halved = folded[:]
+                        nc.gpsimd.tensor_tensor(
+                            sums[:, NODES - HELPED : NODES].unsqueeze(2),
+                            halved[:, :, 0:1],
+                            halved[:, :, 1:2],
+                            mybir.AluOpType.add,
                         )
                     else:
                         by_edge = of_unit.rearrange("p (m k) -> p k m", k=K)

import concourse.mybir as mybir
from concourse.masks import make_identity

F32 = mybir.dt.float32
U16 = mybir.dt.uint16

P = 128
C, S, M, K = 512, 4096, 512, 16
N = M * K
SCALE = 4.9
NODES = P
UNIT = NODES * K
SPAN = 2 * UNIT
BANK = 512
HELPED = 24
FLOPS = 2 * C * N


def steps_of(b, span):
    if b == 0 and span == 0:
        return [0, BANK, UNIT, SPAN]
    if b == C // P - 1 and span == N // SPAN - 1:
        return [0, UNIT, SPAN]
    return [0, SPAN]


def tile_feedforwardnetwork_kernel(tc, x, w, offs, out):
    nc = tc.nc
    with (
        tc.tile_pool(name="held", bufs=1) as held,
        tc.tile_pool(name="work", bufs=3) as work,
        tc.psum_pool(name="psum", bufs=2) as psum,
        tc.psum_pool(name="psum_once", bufs=1) as psum_once,
    ):
        offsets = held.tile([P, N // 16], U16, name="offsets")
        nc.sync.dma_start(offsets[:], offs)
        weight_rows = held.tile([N // P, P], F32, name="weight_rows")
        nc.sync.dma_start(weight_rows[:], w.rearrange("o (q f) -> (o q) f", f=P))
        tables = [held.tile([P, S], F32, name=f"table{b}") for b in range(C // P)]
        for b in range(C // P):
            nc.sync.dma_start(tables[b][:], x[b * P : (b + 1) * P, :])

        identity = held.tile([P, P], F32, name="identity")
        make_identity(nc, identity[:])

        turned = psum_once.tile([P, N // P], F32, name="turned")
        nc.tensor.transpose(turned[:], weight_rows[:], identity[0 : N // P, 0 : N // P])
        weight_columns = held.tile([P, N // P], F32, name="weight_columns")
        nc.scalar.copy(weight_columns[:], turned[:])

        weights = [held.tile([P, SPAN], F32, name=f"weights{span}") for span in range(N // SPAN)]
        for span in range(N // SPAN):
            for bank in range(SPAN // BANK):
                spread = psum.tile([P, BANK], F32, name="spread")
                for part in range(BANK // P):
                    q = (span * SPAN + bank * BANK) // P + part
                    nc.tensor.matmul(
                        spread[:, part * P : (part + 1) * P],
                        lhsT=weight_columns[:, q : q + 1].to_broadcast([P, P]),
                        rhs=identity[:],
                        is_transpose=True,
                        start=True,
                        stop=True,
                    )
                nc.scalar.copy(weights[span][:, bank * BANK : (bank + 1) * BANK], spread[:])

        for span in range(N // SPAN):
            for b in range(C // P):
                products = work.tile([P, SPAN], F32, name="products")
                steps = steps_of(b, span)
                for lo, hi in zip(steps[:-1], steps[1:]):
                    nc.vector.tensor_tensor(
                        products[:, lo:hi],
                        tables[b][:].indirect(offsets[:, (span * SPAN + lo) // 16 : (span * SPAN + hi) // 16]),
                        weights[span][:, lo:hi],
                        mybir.AluOpType.mult,
                    )
                for unit in range(SPAN // UNIT):
                    of_unit = products[:, unit * UNIT : (unit + 1) * UNIT]
                    first_node = (span * SPAN + unit * UNIT) // K
                    if b == C // P - 1 and first_node == M - NODES:
                        by_node = of_unit.rearrange("p (m k) -> p m k", k=K)
                        sums = work.tile([P, NODES], F32, name="last_sums")
                        nc.vector.tensor_reduce(
                            out=sums[:, 0 : NODES - HELPED],
                            in_=by_node[:, 0 : NODES - HELPED, :],
                            axis=mybir.AxisListType.X,
                            op=mybir.AluOpType.add,
                        )
                        halved = by_node[:, NODES - HELPED : NODES, :]
                        for width in (8, 4, 2):
                            folded = work.tile([P, HELPED, width], F32, name=f"folded{width}")
                            nc.gpsimd.tensor_tensor(
                                folded[:],
                                halved[:, :, 0:width],
                                halved[:, :, width : 2 * width],
                                mybir.AluOpType.add,
                            )
                            halved = folded[:]
                        nc.gpsimd.tensor_tensor(
                            sums[:, NODES - HELPED : NODES].unsqueeze(2),
                            halved[:, :, 0:1],
                            halved[:, :, 1:2],
                            mybir.AluOpType.add,
                        )
                    else:
                        by_edge = of_unit.rearrange("p (m k) -> p k m", k=K)
                        sums_by_node = psum.tile([NODES, P], F32, name="sums_by_node")
                        for k in range(K):
                            nc.tensor.matmul(
                                sums_by_node[:],
                                lhsT=by_edge[:, k, :],
                                rhs=identity[:],
                                is_transpose=True,
                                start=(k == 0),
                                stop=(k == K - 1),
                            )
                        sums_copy = work.tile([NODES, P], F32, name="sums_copy")
                        nc.scalar.copy(sums_copy[:], sums_by_node[:])
                        sums = psum.tile([P, NODES], F32, name="sums")
                        nc.tensor.transpose(sums[:], sums_copy[:], identity[:])
                    result = work.tile([P, NODES], F32, name="result")
                    nc.scalar.activation(
                        result[:], sums[:], mybir.ActivationFunctionType.Sigmoid, scale=SCALE
                    )
                    nc.scalar.dma_start(
                        out[b * P : (b + 1) * P, first_node : first_node + NODES], result[:]
                    )
